import numpy as np
import ml_dtypes


def mxq(x, axis, fmt="e4m3"):
    dtype, down = {"e4m3": (ml_dtypes.float8_e4m3fn, 7), "e5m2": (ml_dtypes.float8_e5m2, 14)}[fmt]
    v = np.moveaxis(np.asarray(x, np.float32).astype(ml_dtypes.bfloat16).astype(np.float64), axis, -1)
    blocks = v.reshape(v.shape[:-1] + (-1, 32))
    amax = np.abs(blocks).max(-1, keepdims=True)
    byte = np.maximum(np.where(amax > 0, np.frexp(amax)[1] - 1 + 127, 0) - down, 1)
    scale = np.exp2(byte - 127.0)
    codes = (blocks / scale).astype(np.float32).astype(dtype).astype(np.float64)
    return np.moveaxis((codes * scale).reshape(v.shape), -1, axis)


WIDE = False


def mx_kscale(k):
    if not WIDE:
        return np.ones(k)
    levels = np.array([10, -10, 5, -5, 0])
    a = np.random.permutation(np.resize(levels, k // 512 * 4)).reshape(k // 512, 4)
    idx = np.arange(k)
    return np.exp2(a[idx // 512, idx % 128 // 32])


BF16 = ml_dtypes.bfloat16


def bf(x):
    return np.asarray(x, np.float32).astype(BF16)


def f64(x):
    return np.asarray(x).astype(np.float64)


B, C_IN, N, L, C_OUT, ORDER, EMBED, SUP_LEN = 16, 32, 512, 12, 64, 3, 10, 2


def setup_inputs():
    s = mx_kscale(N)
    return {"a": bf(np.random.standard_normal((N, N)) / np.sqrt(N) * s[None, :] / s[:, None]),
            "x": bf(np.random.standard_normal((B, C_IN, N, L)) / s[None, None, :, None])}


def reference(a, x):
    a, x = f64(a), f64(x)
    a_left = mxq(a, 1, "e4m3")
    xq = mxq(x, 2, "e4m3")
    t2 = 2.0 * (a_left @ mxq(a, 0, "e4m3")) - np.eye(N)
    y1 = a_left @ xq
    y2 = mxq(t2, 1, "e4m3") @ xq
    return np.stack([y1, y2], axis=1).transpose(0, 1, 3, 2, 4)

@@ -1,0 +1,175 @@
+from contextlib import ExitStack
+
+import concourse.mybir as mybir
+from concourse.masks import make_identity
+
+F32 = mybir.dt.float32
+BF16 = mybir.dt.bfloat16
+U32 = mybir.dt.uint32
+U8 = mybir.dt.uint8
+FP8X4 = mybir.dt.float8_e4m3fn_x4
+ALU = mybir.AluOpType
+
+P = 128
+NODES = 512
+B = 16
+C = 32
+L = 12
+CL = C * L
+GROUPS = 4
+B_PER_G = 4
+COLS_G = P * L
+
+FLOPS = 2 * NODES * NODES * NODES + 2 * 2 * NODES * NODES * B * CL
+
+
+def tile_gcn_pa_t_kernel(tc, a, x, out):
+    nc = tc.nc
+    with ExitStack() as ctx:
+        keep = ctx.enter_context(tc.tile_pool(name="keep", bufs=1))
+        xgp = ctx.enter_context(tc.tile_pool(name="xgp", bufs=2))
+        stp = ctx.enter_context(tc.tile_pool(name="stp", bufs=8))
+        pst = ctx.enter_context(tc.psum_pool(name="pst", bufs=3))
+        psy = ctx.enter_context(tc.psum_pool(name="psy", bufs=5))
+
+        a_sb = keep.tile([P, 4 * NODES], BF16, name="a_sb")
+        nc.sync.dma_start(out=a_sb[:], in_=a.rearrange("(p j) m -> p (j m)", j=4))
+        x_rows = x.rearrange("b c m l -> (b c) (m l)")
+        x_sb = []
+        for g in range(GROUPS):
+            xs = keep.tile([P, NODES * L], BF16, name="x_sb%d" % g)
+            nc.sync.dma_start(out=xs[:], in_=x_rows[g * P:(g + 1) * P, :])
+            x_sb.append(xs)
+
+        ident = keep.tile([P, P], F32, name="ident")
+        make_identity(nc, ident[:])
+        eye = keep.tile([P, 4 * P * 4], F32, name="eye")
+        eye_v = eye[:].rearrange("p (j q t) -> p j q t", j=4, t=4)
+        nc.vector.memset(eye[:], 0.0)
+        for j in range(4):
+            nc.vector.tensor_copy(out=eye_v[:, j, :, j], in_=ident[:])
+
+        al_g = keep.tile([P, 4 * NODES], BF16, name="al_g", align_bytes=64)
+        al_c = keep.tile([P, NODES], U32, name="al_c", align_bytes=64)
+        al_s = keep.tile([P, NODES], U8, name="al_s", align_bytes=64)
+        a_words = a_sb[:].bitcast(F32).rearrange("q (j p u) -> q j p u", j=4, u=2)
+        al_words = al_g[:].bitcast(F32).rearrange("p (j q u) -> p j q u", j=4, u=2)
+        for h in range(2):
+            aps = pst.tile([P, 512], F32, name="aps", tag="tp")
+            for jj in range(2):
+                for u in range(2):
+                    nc.tensor.transpose(
+                        aps[:, (2 * jj + u) * P:(2 * jj + u + 1) * P],
+                        a_words[:, 2 * h + jj, :, u],
+                        ident[:],
+                    )
+            src = aps[:].rearrange("p (j u q) -> p j q u", j=2, u=2)
+            if h == 0:
+                nc.vector.tensor_copy(out=al_words[:, 0:2, :, :], in_=src)
+            else:
+                nc.scalar.copy(out=al_words[:, 2:4, :, :], in_=src)
+
+        ar_g = keep.tile([P, 4 * NODES], BF16, name="ar_g", align_bytes=64)
+        ar_c = keep.tile([P, NODES], U32, name="ar_c", align_bytes=64)
+        ar_s = keep.tile([P, NODES], U8, name="ar_s", align_bytes=64)
+        nc.vector.tensor_copy(
+            out=ar_g[:].rearrange("p (s q t) -> p s q t", s=4, t=4),
+            in_=a_sb[:].rearrange("p (t q s) -> p s q t", t=4, s=4),
+        )
+        nc.vector.quantize_mx(out=al_c[:].bitcast(FP8X4), scales=al_s[:], in_=al_g[:])
+        nc.vector.quantize_mx(out=ar_c[:].bitcast(FP8X4), scales=ar_s[:], in_=ar_g[:])
+
+        x_c = []
+        x_s = []
+
+        def xprep(g):
+            xg = xgp.tile([P, 4 * COLS_G], BF16, name="xg", align_bytes=64)
+            xg_v = xg[:].rearrange("p (q l t) -> p q l t", l=L, t=4)
+            xw = x_sb[g][:].bitcast(F32).rearrange("q (p t i) -> q p t i", t=4, i=6)
+            for i in range(6):
+                xps = pst.tile([P, 512], F32, name="xps", tag="tp")
+                for t in range(4):
+                    nc.tensor.transpose(xps[:, t * P:(t + 1) * P], xw[:, :, t, i], ident[:])
+                src = xps[:].bitcast(BF16).rearrange("p (t q e) -> p q e t", t=4, e=2)
+                dst = xg_v[:, :, 2 * i:2 * i + 2, :]
+                on_vector = (i // 2 == 0) or (i // 2 == 2 and g % 2 == 0)
+                if on_vector:
+                    nc.vector.tensor_copy(out=dst, in_=src)
+                else:
+                    nc.scalar.copy(out=dst, in_=src)
+            xc = keep.tile([P, COLS_G], U32, name="x_c%d" % g, align_bytes=64)
+            xs = keep.tile([P, COLS_G], U8, name="x_s%d" % g, align_bytes=64)
+            for s in range(3):
+                nc.vector.quantize_mx(
+                    out=xc[:, s * 512:(s + 1) * 512].bitcast(FP8X4),
+                    scales=xs[:, s * 512:(s + 1) * 512],
+                    in_=xg[:, s * 2048:(s + 1) * 2048],
+                )
+            x_c.append(xc)
+            x_s.append(xs)
+
+        xprep(0)
+
+        t2_g = keep.tile([P, 4 * NODES], BF16, name="t2_g", align_bytes=64)
+        t2_c = keep.tile([P, NODES], U32, name="t2_c", align_bytes=64)
+        t2_s = keep.tile([P, NODES], U8, name="t2_s", align_bytes=64)
+        t2_v = t2_g[:].rearrange("p (j q t) -> p j q t", j=4, t=4)
+        for j in range(4):
+            tps = psy.tile([P, 512], F32, name="tps", tag="y")
+            for s in range(4):
+                nc.tensor.matmul_mx(
+                    out=tps[:, s * P:(s + 1) * P],
+                    lhsT=ar_c[:, s * P:(s + 1) * P].bitcast(FP8X4),
+                    lhsT_scale=ar_s[:, s * P:(s + 1) * P],
+                    rhs=al_c[:, j * P:(j + 1) * P].bitcast(FP8X4),
+                    rhs_scale=al_s[:, j * P:(j + 1) * P],
+                    start=True,
+                    stop=True,
+                )
+            nc.vector.scalar_tensor_tensor(
+                out=t2_v[:, j, :, :],
+                in0=tps[:].rearrange("p (t q) -> p q t", t=4),
+                scalar=2.0,
+                in1=eye_v[:, j, :, :],
+                op0=ALU.mult,
+                op1=ALU.subtract,
+            )
+        nc.vector.quantize_mx(out=t2_c[:].bitcast(FP8X4), scales=t2_s[:], in_=t2_g[:])
+
+        weights = [(al_c, al_s), (t2_c, t2_s)]
+        count = [0]
+
+        def unit(g, bl, term):
+            wc, ws = weights[term]
+            b = g * B_PER_G + bl
+            stage = stp.tile([P, 4 * CL], F32, name="stage")
+            for j in range(4):
+                yps = psy.tile([P, 512], F32, name="yps", tag="y")
+                for lo, n in ((0, 256), (256, 128)):
+                    c0 = bl * CL + lo
+                    nc.tensor.matmul_mx(
+                        out=yps[:, lo:lo + n],
+                        lhsT=wc[:, j * P:(j + 1) * P].bitcast(FP8X4),
+                        lhsT_scale=ws[:, j * P:(j + 1) * P],
+                        rhs=x_c[g][:, c0:c0 + n].bitcast(FP8X4),
+                        rhs_scale=x_s[g][:, c0:c0 + n],
+                        start=True,
+                        stop=True,
+                    )
+                k = count[0] % 16
+                count[0] += 1
+                if k % 2 == 0 and k != 14:
+                    nc.vector.tensor_copy(out=stage[:, j * CL:(j + 1) * CL], in_=yps[:, 0:CL])
+                else:
+                    nc.scalar.copy(out=stage[:, j * CL:(j + 1) * CL], in_=yps[:, 0:CL])
+            nc.sync.dma_start(
+                out=out[b, term].rearrange("(p j) c l -> p (j c l)", j=4), in_=stage[:]
+            )
+
+        for g in range(GROUPS):
+            for bl in range(B_PER_G):
+                unit(g, bl, 0)
+            if g + 1 < GROUPS:
+                xprep(g + 1)
+            for bl in range(B_PER_G):
+                unit(g, bl, 1)

@@ -19,6 +19,8 @@ CL = C * L
 GROUPS = 4
 B_PER_G = 4
 COLS_G = P * L
+XHALF = 490.0
+YCOPY = 380.0
 
 FLOPS = 2 * NODES * NODES * NODES + 2 * 2 * NODES * NODES * B * CL
 
@@ -28,9 +30,8 @@ def tile_gcn_pa_t_kernel(tc, a, x, out):
     with ExitStack() as ctx:
         keep = ctx.enter_context(tc.tile_pool(name="keep", bufs=1))
         xgp = ctx.enter_context(tc.tile_pool(name="xgp", bufs=2))
-        stp = ctx.enter_context(tc.tile_pool(name="stp", bufs=8))
-        pst = ctx.enter_context(tc.psum_pool(name="pst", bufs=3))
-        psy = ctx.enter_context(tc.psum_pool(name="psy", bufs=5))
+        stp = ctx.enter_context(tc.tile_pool(name="stp", bufs=12))
+        psum = ctx.enter_context(tc.psum_pool(name="psum", bufs=8))
 
         a_sb = keep.tile([P, 4 * NODES], BF16, name="a_sb")
         nc.sync.dma_start(out=a_sb[:], in_=a.rearrange("(p j) m -> p (j m)", j=4))
@@ -52,10 +53,32 @@ def tile_gcn_pa_t_kernel(tc, a, x, out):
         al_g = keep.tile([P, 4 * NODES], BF16, name="al_g", align_bytes=64)
         al_c = keep.tile([P, NODES], U32, name="al_c", align_bytes=64)
         al_s = keep.tile([P, NODES], U8, name="al_s", align_bytes=64)
+        ar_g = keep.tile([P, 4 * NODES], BF16, name="ar_g", align_bytes=64)
+        ar_c = keep.tile([P, NODES], U32, name="ar_c", align_bytes=64)
+        ar_s = keep.tile([P, NODES], U8, name="ar_s", align_bytes=64)
+        t2_g = keep.tile([P, 4 * NODES], BF16, name="t2_g", align_bytes=64)
+        t2_c = keep.tile([P, NODES], U32, name="t2_c", align_bytes=64)
+        t2_s = keep.tile([P, NODES], U8, name="t2_s", align_bytes=64)
+        x_c = []
+        x_s = []
+        for g in range(GROUPS):
+            xc = keep.tile([P, COLS_G], U32, name="x_c%d" % g, align_bytes=64)
+            xsc = keep.tile([P, COLS_G], U8, name="x_s%d" % g, align_bytes=64)
+            x_c.append(xc)
+            x_s.append(xsc)
+        weights = [(al_c, al_s), (t2_c, t2_s)]
+        busy = [0.0, 0.0]
+        ctx.enter_context(tc.manual_schedule())
+
+        nc.vector.tensor_copy(
+            out=ar_g[:].rearrange("p (s q t) -> p s q t", s=4, t=4),
+            in_=a_sb[:].rearrange("p (t q s) -> p s q t", t=4, s=4),
+        )
         a_words = a_sb[:].bitcast(F32).rearrange("q (j p u) -> q j p u", j=4, u=2)
         al_words = al_g[:].bitcast(F32).rearrange("p (j q u) -> p j q u", j=4, u=2)
+        a_banks = []
         for h in range(2):
-            aps = pst.tile([P, 512], F32, name="aps", tag="tp")
+            aps = psum.tile([P, 512], F32, name="aps", tag="bank")
             for jj in range(2):
                 for u in range(2):
                     nc.tensor.transpose(
@@ -63,88 +86,50 @@ def tile_gcn_pa_t_kernel(tc, a, x, out):
                         a_words[:, 2 * h + jj, :, u],
                         ident[:],
                     )
-            src = aps[:].rearrange("p (j u q) -> p j q u", j=2, u=2)
-            if h == 0:
-                nc.vector.tensor_copy(out=al_words[:, 0:2, :, :], in_=src)
-            else:
-                nc.scalar.copy(out=al_words[:, 2:4, :, :], in_=src)
-
-        ar_g = keep.tile([P, 4 * NODES], BF16, name="ar_g", align_bytes=64)
-        ar_c = keep.tile([P, NODES], U32, name="ar_c", align_bytes=64)
-        ar_s = keep.tile([P, NODES], U8, name="ar_s", align_bytes=64)
+            a_banks.append(aps)
         nc.vector.tensor_copy(
-            out=ar_g[:].rearrange("p (s q t) -> p s q t", s=4, t=4),
-            in_=a_sb[:].rearrange("p (t q s) -> p s q t", t=4, s=4),
+            out=al_words[:, 0:2, :, :], in_=a_banks[0][:].rearrange("p (j u q) -> p j q u", j=2, u=2)
+        )
+        nc.scalar.copy(
+            out=al_words[:, 2:4, :, :], in_=a_banks[1][:].rearrange("p (j u q) -> p j q u", j=2, u=2)
         )
         nc.vector.quantize_mx(out=al_c[:].bitcast(FP8X4), scales=al_s[:], in_=al_g[:])
         nc.vector.quantize_mx(out=ar_c[:].bitcast(FP8X4), scales=ar_s[:], in_=ar_g[:])
 
-        x_c = []
-        x_s = []
+        xg_of = {}
 
-        def xprep(g):
-            xg = xgp.tile([P, 4 * COLS_G], BF16, name="xg", align_bytes=64)
-            xg_v = xg[:].rearrange("p (q l t) -> p q l t", l=L, t=4)
+        def x_bank(g, i):
+            if i == 0:
+                xg_new = xgp.tile([P, 4 * COLS_G], BF16, name="xg", align_bytes=64)
+                xg_of[g] = xg_new
+            xg_v = xg_of[g][:].rearrange("p (q l t) -> p q l t", l=L, t=4)
             xw = x_sb[g][:].bitcast(F32).rearrange("q (p t i) -> q p t i", t=4, i=6)
-            for i in range(6):
-                xps = pst.tile([P, 512], F32, name="xps", tag="tp")
-                for t in range(4):
-                    nc.tensor.transpose(xps[:, t * P:(t + 1) * P], xw[:, :, t, i], ident[:])
-                src = xps[:].bitcast(BF16).rearrange("p (t q e) -> p q e t", t=4, e=2)
-                dst = xg_v[:, :, 2 * i:2 * i + 2, :]
-                on_vector = (i // 2 == 0) or (i // 2 == 2 and g % 2 == 0)
-                if on_vector:
-                    nc.vector.tensor_copy(out=dst, in_=src)
-                else:
-                    nc.scalar.copy(out=dst, in_=src)
-            xc = keep.tile([P, COLS_G], U32, name="x_c%d" % g, align_bytes=64)
-            xs = keep.tile([P, COLS_G], U8, name="x_s%d" % g, align_bytes=64)
-            for s in range(3):
+            xps = psum.tile([P, 512], F32, name="xps", tag="bank")
+            for t in range(4):
+                nc.tensor.transpose(xps[:, t * P:(t + 1) * P], xw[:, :, t, i], ident[:])
+            src = xps[:].bitcast(BF16).rearrange("p (t q e) -> p q e t", t=4, e=2)
+            nc.vector.tensor_copy(out=xg_v[:, 0:64, 2 * i:2 * i + 2, :], in_=src[:, 0:64, :, :])
+            nc.scalar.copy(out=xg_v[:, 64:128, 2 * i:2 * i + 2, :], in_=src[:, 64:128, :, :])
+            busy[0] += XHALF
+            busy[1] += XHALF
+
+        def x_quant(g, half):
+            for w0, wn in (((0, 512), (512, 256)), ((768, 256), (1024, 512)))[half]:
                 nc.vector.quantize_mx(
-                    out=xc[:, s * 512:(s + 1) * 512].bitcast(FP8X4),
-                    scales=xs[:, s * 512:(s + 1) * 512],
-                    in_=xg[:, s * 2048:(s + 1) * 2048],
+                    out=x_c[g][:, w0:w0 + wn].bitcast(FP8X4),
+                    scales=x_s[g][:, w0:w0 + wn],
+                    in_=xg_of[g][:, 4 * w0:4 * (w0 + wn)],
                 )
-            x_c.append(xc)
-            x_s.append(xs)
+                busy[0] += 12 + 0.88 * wn
 
-        xprep(0)
-
-        t2_g = keep.tile([P, 4 * NODES], BF16, name="t2_g", align_bytes=64)
-        t2_c = keep.tile([P, NODES], U32, name="t2_c", align_bytes=64)
-        t2_s = keep.tile([P, NODES], U8, name="t2_s", align_bytes=64)
-        t2_v = t2_g[:].rearrange("p (j q t) -> p j q t", j=4, t=4)
-        for j in range(4):
-            tps = psy.tile([P, 512], F32, name="tps", tag="y")
-            for s in range(4):
-                nc.tensor.matmul_mx(
-                    out=tps[:, s * P:(s + 1) * P],
-                    lhsT=ar_c[:, s * P:(s + 1) * P].bitcast(FP8X4),
-                    lhsT_scale=ar_s[:, s * P:(s + 1) * P],
-                    rhs=al_c[:, j * P:(j + 1) * P].bitcast(FP8X4),
-                    rhs_scale=al_s[:, j * P:(j + 1) * P],
-                    start=True,
-                    stop=True,
-                )
-            nc.vector.scalar_tensor_tensor(
-                out=t2_v[:, j, :, :],
-                in0=tps[:].rearrange("p (t q) -> p q t", t=4),
-                scalar=2.0,
-                in1=eye_v[:, j, :, :],
-                op0=ALU.mult,
-                op1=ALU.subtract,
-            )
-        nc.vector.quantize_mx(out=t2_c[:].bitcast(FP8X4), scales=t2_s[:], in_=t2_g[:])
-
-        weights = [(al_c, al_s), (t2_c, t2_s)]
-        count = [0]
-
-        def unit(g, bl, term):
+        def unit(g, u):
+            term = u // B_PER_G
+            bl = u % B_PER_G
             wc, ws = weights[term]
             b = g * B_PER_G + bl
             stage = stp.tile([P, 4 * CL], F32, name="stage")
             for j in range(4):
-                yps = psy.tile([P, 512], F32, name="yps", tag="y")
+                yps = psum.tile([P, 512], F32, name="yps", tag="bank")
                 for lo, n in ((0, 256), (256, 128)):
                     c0 = bl * CL + lo
                     nc.tensor.matmul_mx(
@@ -156,20 +141,57 @@ def tile_gcn_pa_t_kernel(tc, a, x, out):
                         start=True,
                         stop=True,
                     )
-                k = count[0] % 16
-                count[0] += 1
-                if k % 2 == 0 and k != 14:
+                if busy[0] < busy[1]:
                     nc.vector.tensor_copy(out=stage[:, j * CL:(j + 1) * CL], in_=yps[:, 0:CL])
+                    busy[0] += YCOPY
                 else:
                     nc.scalar.copy(out=stage[:, j * CL:(j + 1) * CL], in_=yps[:, 0:CL])
+                    busy[1] += YCOPY
             nc.sync.dma_start(
                 out=out[b, term].rearrange("(p j) c l -> p (j c l)", j=4), in_=stage[:]
             )
 
+        for i in range(6):
+            x_bank(0, i)
+
+        t2_v = t2_g[:].rearrange("p (j q t) -> p j q t", j=4, t=4)
+        t_banks = []
+        for j in range(4):
+            tps = psum.tile([P, 512], F32, name="tps", tag="bank")
+            for s in range(4):
+                nc.tensor.matmul_mx(
+                    out=tps[:, s * P:(s + 1) * P],
+                    lhsT=ar_c[:, s * P:(s + 1) * P].bitcast(FP8X4),
+                    lhsT_scale=ar_s[:, s * P:(s + 1) * P],
+                    rhs=al_c[:, j * P:(j + 1) * P].bitcast(FP8X4),
+                    rhs_scale=al_s[:, j * P:(j + 1) * P],
+                    start=True,
+                    stop=True,
+                )
+            t_banks.append(tps)
+        x_quant(0, 0)
+        for j in range(4):
+            nc.vector.scalar_tensor_tensor(
+                out=t2_v[:, j, :, :],
+                in0=t_banks[j][:].rearrange("p (t q) -> p q t", t=4),
+                scalar=2.0,
+                in1=eye_v[:, j, :, :],
+                op0=ALU.mult,
+                op1=ALU.subtract,
+            )
+            busy[0] += XHALF
+        x_quant(0, 1)
+        nc.vector.quantize_mx(out=t2_c[:].bitcast(FP8X4), scales=t2_s[:], in_=t2_g[:])
+        busy[0] += 12 + 0.88 * 512
+
         for g in range(GROUPS):
-            for bl in range(B_PER_G):
-                unit(g, bl, 0)
-            if g + 1 < GROUPS:
-                xprep(g + 1)
-            for bl in range(B_PER_G):
-                unit(g, bl, 1)
+            more = g + 1 < GROUPS
+            for u in range(2 * B_PER_G):
+                unit(g, u)
+                if more and u in (1, 3, 5):
+                    x_bank(g + 1, u - 1)
+                    x_bank(g + 1, u)
+                if more and u == 5:
+                    x_quant(g + 1, 0)
+                if more and u == 6:
+                    x_quant(g + 1, 1)

@@ -19,7 +19,7 @@ CL = C * L
 GROUPS = 4
 B_PER_G = 4
 COLS_G = P * L
-XHALF = 490.0
+XCOPY = 490.0
 YCOPY = 380.0
 
 FLOPS = 2 * NODES * NODES * NODES + 2 * 2 * NODES * NODES * B * CL
@@ -29,7 +29,8 @@ def tile_gcn_pa_t_kernel(tc, a, x, out):
     nc = tc.nc
     with ExitStack() as ctx:
         keep = ctx.enter_context(tc.tile_pool(name="keep", bufs=1))
-        xgp = ctx.enter_context(tc.tile_pool(name="xgp", bufs=2))
+        xgp = ctx.enter_context(tc.tile_pool(name="xgp", bufs=1))
+        x2p = ctx.enter_context(tc.tile_pool(name="x2p", bufs=2))
         stp = ctx.enter_context(tc.tile_pool(name="stp", bufs=12))
         psum = ctx.enter_context(tc.psum_pool(name="psum", bufs=8))
 
@@ -70,38 +71,30 @@ def tile_gcn_pa_t_kernel(tc, a, x, out):
         busy = [0.0, 0.0]
         ctx.enter_context(tc.manual_schedule())
 
-        nc.vector.tensor_copy(
-            out=ar_g[:].rearrange("p (s q t) -> p s q t", s=4, t=4),
-            in_=a_sb[:].rearrange("p (t q s) -> p s q t", t=4, s=4),
-        )
-        a_words = a_sb[:].bitcast(F32).rearrange("q (j p u) -> q j p u", j=4, u=2)
-        al_words = al_g[:].bitcast(F32).rearrange("p (j q u) -> p j q u", j=4, u=2)
-        a_banks = []
-        for h in range(2):
-            aps = psum.tile([P, 512], F32, name="aps", tag="bank")
-            for jj in range(2):
-                for u in range(2):
-                    nc.tensor.transpose(
-                        aps[:, (2 * jj + u) * P:(2 * jj + u + 1) * P],
-                        a_words[:, 2 * h + jj, :, u],
-                        ident[:],
-                    )
-            a_banks.append(aps)
-        nc.vector.tensor_copy(
-            out=al_words[:, 0:2, :, :], in_=a_banks[0][:].rearrange("p (j u q) -> p j q u", j=2, u=2)
-        )
-        nc.scalar.copy(
-            out=al_words[:, 2:4, :, :], in_=a_banks[1][:].rearrange("p (j u q) -> p j q u", j=2, u=2)
-        )
-        nc.vector.quantize_mx(out=al_c[:].bitcast(FP8X4), scales=al_s[:], in_=al_g[:])
-        nc.vector.quantize_mx(out=ar_c[:].bitcast(FP8X4), scales=ar_s[:], in_=ar_g[:])
-
+        x2_of = {}
         xg_of = {}
 
-        def x_bank(g, i):
-            if i == 0:
-                xg_new = xgp.tile([P, 4 * COLS_G], BF16, name="xg", align_bytes=64)
-                xg_of[g] = xg_new
+        def presort(g):
+            x2 = x2p.tile([P, NODES * L], BF16, name="x2")
+            x2_of[g] = x2
+            dst = x2[:].rearrange("q (l u p e) -> q l u p e", l=L, u=2, e=2)
+            src = x_sb[g][:].rearrange("q (p u e l) -> q l u p e", u=2, e=2, l=L)
+            for h in range(3):
+                for u in range(2):
+                    nc.gpsimd.tensor_scalar(
+                        out=dst[:, 4 * h:4 * h + 4, u, :, :],
+                        in0=src[:, 4 * h:4 * h + 4, u, :, :],
+                        scalar1=1.0,
+                        scalar2=0.0,
+                        op0=ALU.mult,
+                        op1=ALU.add,
+                    )
+
+        def new_xg(g):
+            xg_new = xgp.tile([P, 4 * COLS_G], BF16, name="xg", align_bytes=64)
+            xg_of[g] = xg_new
+
+        def x_bank_direct(g, i):
             xg_v = xg_of[g][:].rearrange("p (q l t) -> p q l t", l=L, t=4)
             xw = x_sb[g][:].bitcast(F32).rearrange("q (p t i) -> q p t i", t=4, i=6)
             xps = psum.tile([P, 512], F32, name="xps", tag="bank")
@@ -110,8 +103,32 @@ def tile_gcn_pa_t_kernel(tc, a, x, out):
             src = xps[:].bitcast(BF16).rearrange("p (t q e) -> p q e t", t=4, e=2)
             nc.vector.tensor_copy(out=xg_v[:, 0:64, 2 * i:2 * i + 2, :], in_=src[:, 0:64, :, :])
             nc.scalar.copy(out=xg_v[:, 64:128, 2 * i:2 * i + 2, :], in_=src[:, 64:128, :, :])
-            busy[0] += XHALF
-            busy[1] += XHALF
+            busy[0] += XCOPY
+            busy[1] += XCOPY
+
+        def x_pair_sorted(g, h):
+            xg_w = xg_of[g][:].bitcast(F32).rearrange("p (q l u) -> p q l u", l=L, u=2)
+            xw = x2_of[g][:].bitcast(F32).rearrange("q (l u p) -> q l u p", l=L, u=2)
+            banks = []
+            for lp in range(2):
+                xps = psum.tile([P, 512], F32, name="xps", tag="bank")
+                for l2 in range(2):
+                    for u in range(2):
+                        nc.tensor.transpose(
+                            xps[:, (2 * l2 + u) * P:(2 * l2 + u + 1) * P],
+                            xw[:, 4 * h + 2 * lp + l2, u, :],
+                            ident[:],
+                        )
+                banks.append(xps)
+            e = 0 if busy[0] < busy[1] else 1
+            for lp in range(2):
+                l0 = 4 * h + 2 * lp
+                src = banks[lp][:].rearrange("p (l u q) -> p q l u", l=2, u=2)
+                if e == 0:
+                    nc.vector.tensor_copy(out=xg_w[:, :, l0:l0 + 2, :], in_=src)
+                else:
+                    nc.scalar.copy(out=xg_w[:, :, l0:l0 + 2, :], in_=src)
+                busy[e] += XCOPY
 
         def x_quant(g, half):
             for w0, wn in (((0, 512), (512, 256)), ((768, 256), (1024, 512)))[half]:
@@ -151,8 +168,41 @@ def tile_gcn_pa_t_kernel(tc, a, x, out):
                 out=out[b, term].rearrange("(p j) c l -> p (j c l)", j=4), in_=stage[:]
             )
 
+        nc.vector.tensor_copy(
+            out=ar_g[:].rearrange("p (s q t) -> p s q t", s=4, t=4),
+            in_=a_sb[:].rearrange("p (t q s) -> p s q t", t=4, s=4),
+        )
+        a_words = a_sb[:].bitcast(F32).rearrange("q (j p u) -> q j p u", j=4, u=2)
+        al_words = al_g[:].bitcast(F32).rearrange("p (j q u) -> p j q u", j=4, u=2)
+        a_banks = []
+        for h in range(2):
+            aps = psum.tile([P, 512], F32, name="aps", tag="bank")
+            for jj in range(2):
+                for u in range(2):
+                    nc.tensor.transpose(
+                        aps[:, (2 * jj + u) * P:(2 * jj + u + 1) * P],
+                        a_words[:, 2 * h + jj, :, u],
+                        ident[:],
+                    )
+            a_banks.append(aps)
+        nc.vector.tensor_copy(
+            out=al_words[:, 0:2, :, :], in_=a_banks[0][:].rearrange("p (j u q) -> p j q u", j=2, u=2)
+        )
+        nc.scalar.copy(
+            out=al_words[:, 2:4, :, :], in_=a_banks[1][:].rearrange("p (j u q) -> p j q u", j=2, u=2)
+        )
+        nc.vector.quantize_mx(out=al_c[:].bitcast(FP8X4), scales=al_s[:], in_=al_g[:])
+        nc.vector.quantize_mx(out=ar_c[:].bitcast(FP8X4), scales=ar_s[:], in_=ar_g[:])
+
+        presort(1)
+        presort(2)
+        new_xg(0)
         for i in range(6):
-            x_bank(0, i)
+            x_bank_direct(0, i)
+        x_quant(0, 0)
+        unit(0, 0)
+        x_quant(0, 1)
+        unit(0, 1)
 
         t2_v = t2_g[:].rearrange("p (j q t) -> p j q t", j=4, t=4)
         t_banks = []
@@ -169,8 +219,8 @@ def tile_gcn_pa_t_kernel(tc, a, x, out):
                     stop=True,
                 )
             t_banks.append(tps)
-        x_quant(0, 0)
-        for j in range(4):
+
+        def t2_round(j):
             nc.vector.scalar_tensor_tensor(
                 out=t2_v[:, j, :, :],
                 in0=t_banks[j][:].rearrange("p (t q) -> p q t", t=4),
@@ -179,19 +229,31 @@ def tile_gcn_pa_t_kernel(tc, a, x, out):
                 op0=ALU.mult,
                 op1=ALU.subtract,
             )
-            busy[0] += XHALF
-        x_quant(0, 1)
+            busy[0] += XCOPY
+
+        t2_round(0)
+        t2_round(1)
+        unit(0, 2)
+        t2_round(2)
+        t2_round(3)
         nc.vector.quantize_mx(out=t2_c[:].bitcast(FP8X4), scales=t2_s[:], in_=t2_g[:])
         busy[0] += 12 + 0.88 * 512
+        unit(0, 3)
 
         for g in range(GROUPS):
             more = g + 1 < GROUPS
+            pair_after = (3, 4, 5) if g == 0 else (1, 3, 5)
             for u in range(2 * B_PER_G):
-                unit(g, u)
-                if more and u in (1, 3, 5):
-                    x_bank(g + 1, u - 1)
-                    x_bank(g + 1, u)
-                if more and u == 5:
-                    x_quant(g + 1, 0)
+                if g > 0 or u >= B_PER_G:
+                    unit(g, u)
+                if more and u in pair_after:
+                    h = pair_after.index(u)
+                    if h == 0:
+                        new_xg(g + 1)
+                    x_pair_sorted(g + 1, h)
+                    if h == 2:
+                        x_quant(g + 1, 0)
+                        if g + 3 < GROUPS:
+                            presort(g + 3)
                 if more and u == 6:
                     x_quant(g + 1, 1)

@@ -19,7 +19,7 @@ CL = C * L
 GROUPS = 4
 B_PER_G = 4
 COLS_G = P * L
-XCOPY = 490.0
+XHALF = 490.0
 YCOPY = 380.0
 
 FLOPS = 2 * NODES * NODES * NODES + 2 * 2 * NODES * NODES * B * CL
@@ -29,8 +29,7 @@ def tile_gcn_pa_t_kernel(tc, a, x, out):
     nc = tc.nc
     with ExitStack() as ctx:
         keep = ctx.enter_context(tc.tile_pool(name="keep", bufs=1))
-        xgp = ctx.enter_context(tc.tile_pool(name="xgp", bufs=1))
-        x2p = ctx.enter_context(tc.tile_pool(name="x2p", bufs=2))
+        xgp = ctx.enter_context(tc.tile_pool(name="xgp", bufs=2))
         stp = ctx.enter_context(tc.tile_pool(name="stp", bufs=12))
         psum = ctx.enter_context(tc.psum_pool(name="psum", bufs=8))
 
@@ -71,30 +70,38 @@ def tile_gcn_pa_t_kernel(tc, a, x, out):
         busy = [0.0, 0.0]
         ctx.enter_context(tc.manual_schedule())
 
-        x2_of = {}
+        nc.vector.tensor_copy(
+            out=ar_g[:].rearrange("p (s q t) -> p s q t", s=4, t=4),
+            in_=a_sb[:].rearrange("p (t q s) -> p s q t", t=4, s=4),
+        )
+        a_words = a_sb[:].bitcast(F32).rearrange("q (j p u) -> q j p u", j=4, u=2)
+        al_words = al_g[:].bitcast(F32).rearrange("p (j q u) -> p j q u", j=4, u=2)
+        a_banks = []
+        for h in range(2):
+            aps = psum.tile([P, 512], F32, name="aps", tag="bank")
+            for jj in range(2):
+                for u in range(2):
+                    nc.tensor.transpose(
+                        aps[:, (2 * jj + u) * P:(2 * jj + u + 1) * P],
+                        a_words[:, 2 * h + jj, :, u],
+                        ident[:],
+                    )
+            a_banks.append(aps)
+        nc.vector.tensor_copy(
+            out=al_words[:, 0:2, :, :], in_=a_banks[0][:].rearrange("p (j u q) -> p j q u", j=2, u=2)
+        )
+        nc.scalar.copy(
+            out=al_words[:, 2:4, :, :], in_=a_banks[1][:].rearrange("p (j u q) -> p j q u", j=2, u=2)
+        )
+        nc.vector.quantize_mx(out=al_c[:].bitcast(FP8X4), scales=al_s[:], in_=al_g[:])
+        nc.vector.quantize_mx(out=ar_c[:].bitcast(FP8X4), scales=ar_s[:], in_=ar_g[:])
+
         xg_of = {}
 
-        def presort(g):
-            x2 = x2p.tile([P, NODES * L], BF16, name="x2")
-            x2_of[g] = x2
-            dst = x2[:].rearrange("q (l u p e) -> q l u p e", l=L, u=2, e=2)
-            src = x_sb[g][:].rearrange("q (p u e l) -> q l u p e", u=2, e=2, l=L)
-            for h in range(3):
-                for u in range(2):
-                    nc.gpsimd.tensor_scalar(
-                        out=dst[:, 4 * h:4 * h + 4, u, :, :],
-                        in0=src[:, 4 * h:4 * h + 4, u, :, :],
-                        scalar1=1.0,
-                        scalar2=0.0,
-                        op0=ALU.mult,
-                        op1=ALU.add,
-                    )
-
-        def new_xg(g):
-            xg_new = xgp.tile([P, 4 * COLS_G], BF16, name="xg", align_bytes=64)
-            xg_of[g] = xg_new
-
-        def x_bank_direct(g, i):
+        def x_bank(g, i):
+            if i == 0:
+                xg_new = xgp.tile([P, 4 * COLS_G], BF16, name="xg", align_bytes=64)
+                xg_of[g] = xg_new
             xg_v = xg_of[g][:].rearrange("p (q l t) -> p q l t", l=L, t=4)
             xw = x_sb[g][:].bitcast(F32).rearrange("q (p t i) -> q p t i", t=4, i=6)
             xps = psum.tile([P, 512], F32, name="xps", tag="bank")
@@ -103,32 +110,8 @@ def tile_gcn_pa_t_kernel(tc, a, x, out):
             src = xps[:].bitcast(BF16).rearrange("p (t q e) -> p q e t", t=4, e=2)
             nc.vector.tensor_copy(out=xg_v[:, 0:64, 2 * i:2 * i + 2, :], in_=src[:, 0:64, :, :])
             nc.scalar.copy(out=xg_v[:, 64:128, 2 * i:2 * i + 2, :], in_=src[:, 64:128, :, :])
-            busy[0] += XCOPY
-            busy[1] += XCOPY
-
-        def x_pair_sorted(g, h):
-            xg_w = xg_of[g][:].bitcast(F32).rearrange("p (q l u) -> p q l u", l=L, u=2)
-            xw = x2_of[g][:].bitcast(F32).rearrange("q (l u p) -> q l u p", l=L, u=2)
-            banks = []
-            for lp in range(2):
-                xps = psum.tile([P, 512], F32, name="xps", tag="bank")
-                for l2 in range(2):
-                    for u in range(2):
-                        nc.tensor.transpose(
-                            xps[:, (2 * l2 + u) * P:(2 * l2 + u + 1) * P],
-                            xw[:, 4 * h + 2 * lp + l2, u, :],
-                            ident[:],
-                        )
-                banks.append(xps)
-            e = 0 if busy[0] < busy[1] else 1
-            for lp in range(2):
-                l0 = 4 * h + 2 * lp
-                src = banks[lp][:].rearrange("p (l u q) -> p q l u", l=2, u=2)
-                if e == 0:
-                    nc.vector.tensor_copy(out=xg_w[:, :, l0:l0 + 2, :], in_=src)
-                else:
-                    nc.scalar.copy(out=xg_w[:, :, l0:l0 + 2, :], in_=src)
-                busy[e] += XCOPY
+            busy[0] += XHALF
+            busy[1] += XHALF
 
         def x_quant(g, half):
             for w0, wn in (((0, 512), (512, 256)), ((768, 256), (1024, 512)))[half]:
@@ -168,41 +151,8 @@ def tile_gcn_pa_t_kernel(tc, a, x, out):
                 out=out[b, term].rearrange("(p j) c l -> p (j c l)", j=4), in_=stage[:]
             )
 
-        nc.vector.tensor_copy(
-            out=ar_g[:].rearrange("p (s q t) -> p s q t", s=4, t=4),
-            in_=a_sb[:].rearrange("p (t q s) -> p s q t", t=4, s=4),
-        )
-        a_words = a_sb[:].bitcast(F32).rearrange("q (j p u) -> q j p u", j=4, u=2)
-        al_words = al_g[:].bitcast(F32).rearrange("p (j q u) -> p j q u", j=4, u=2)
-        a_banks = []
-        for h in range(2):
-            aps = psum.tile([P, 512], F32, name="aps", tag="bank")
-            for jj in range(2):
-                for u in range(2):
-                    nc.tensor.transpose(
-                        aps[:, (2 * jj + u) * P:(2 * jj + u + 1) * P],
-                        a_words[:, 2 * h + jj, :, u],
-                        ident[:],
-                    )
-            a_banks.append(aps)
-        nc.vector.tensor_copy(
-            out=al_words[:, 0:2, :, :], in_=a_banks[0][:].rearrange("p (j u q) -> p j q u", j=2, u=2)
-        )
-        nc.scalar.copy(
-            out=al_words[:, 2:4, :, :], in_=a_banks[1][:].rearrange("p (j u q) -> p j q u", j=2, u=2)
-        )
-        nc.vector.quantize_mx(out=al_c[:].bitcast(FP8X4), scales=al_s[:], in_=al_g[:])
-        nc.vector.quantize_mx(out=ar_c[:].bitcast(FP8X4), scales=ar_s[:], in_=ar_g[:])
-
-        presort(1)
-        presort(2)
-        new_xg(0)
         for i in range(6):
-            x_bank_direct(0, i)
-        x_quant(0, 0)
-        unit(0, 0)
-        x_quant(0, 1)
-        unit(0, 1)
+            x_bank(0, i)
 
         t2_v = t2_g[:].rearrange("p (j q t) -> p j q t", j=4, t=4)
         t_banks = []
@@ -219,8 +169,8 @@ def tile_gcn_pa_t_kernel(tc, a, x, out):
                     stop=True,
                 )
             t_banks.append(tps)
-
-        def t2_round(j):
+        x_quant(0, 0)
+        for j in range(4):
             nc.vector.scalar_tensor_tensor(
                 out=t2_v[:, j, :, :],
                 in0=t_banks[j][:].rearrange("p (t q) -> p q t", t=4),
@@ -229,31 +179,21 @@ def tile_gcn_pa_t_kernel(tc, a, x, out):
                 op0=ALU.mult,
                 op1=ALU.subtract,
             )
-            busy[0] += XCOPY
-
-        t2_round(0)
-        t2_round(1)
-        unit(0, 2)
-        t2_round(2)
-        t2_round(3)
+            busy[0] += XHALF
+        x_quant(0, 1)
         nc.vector.quantize_mx(out=t2_c[:].bitcast(FP8X4), scales=t2_s[:], in_=t2_g[:])
         busy[0] += 12 + 0.88 * 512
-        unit(0, 3)
 
         for g in range(GROUPS):
             more = g + 1 < GROUPS
-            pair_after = (3, 4, 5) if g == 0 else (1, 3, 5)
             for u in range(2 * B_PER_G):
-                if g > 0 or u >= B_PER_G:
-                    unit(g, u)
+                unit(g, u)
+                pair_after = (3, 5, 6) if g == 0 else (1, 3, 5)
                 if more and u in pair_after:
                     h = pair_after.index(u)
-                    if h == 0:
-                        new_xg(g + 1)
-                    x_pair_sorted(g + 1, h)
+                    x_bank(g + 1, 2 * h)
+                    x_bank(g + 1, 2 * h + 1)
                     if h == 2:
                         x_quant(g + 1, 0)
-                        if g + 3 < GROUPS:
-                            presort(g + 3)
-                if more and u == 6:
+                if more and u == pair_after[2] + 1:
                     x_quant(g + 1, 1)

@@ -16,11 +16,8 @@ B = 16
 C = 32
 L = 12
 CL = C * L
-GROUPS = 4
-B_PER_G = 4
-COLS_G = P * L
-XHALF = 490.0
-YCOPY = 380.0
+WIDE = 256
+NARROW = CL - WIDE
 
 FLOPS = 2 * NODES * NODES * NODES + 2 * 2 * NODES * NODES * B * CL
 
@@ -29,26 +26,30 @@ def tile_gcn_pa_t_kernel(tc, a, x, out):
     nc = tc.nc
     with ExitStack() as ctx:
         keep = ctx.enter_context(tc.tile_pool(name="keep", bufs=1))
-        xgp = ctx.enter_context(tc.tile_pool(name="xgp", bufs=2))
+        xgp = ctx.enter_context(tc.tile_pool(name="xgp", bufs=3))
         stp = ctx.enter_context(tc.tile_pool(name="stp", bufs=12))
         psum = ctx.enter_context(tc.psum_pool(name="psum", bufs=8))
 
         a_sb = keep.tile([P, 4 * NODES], BF16, name="a_sb")
-        nc.sync.dma_start(out=a_sb[:], in_=a.rearrange("(p j) m -> p (j m)", j=4))
-        x_rows = x.rearrange("b c m l -> (b c) (m l)")
+        nc.sync.dma_start(
+            out=a_sb[:].rearrange("p (t m) -> p t m", t=4), in_=a.rearrange("(t p) m -> p t m", t=4)
+        )
+        x_rows = x.rearrange("b c (t p) l -> b (c t) (p l)", t=4)
         x_sb = []
-        for g in range(GROUPS):
-            xs = keep.tile([P, NODES * L], BF16, name="x_sb%d" % g)
-            nc.sync.dma_start(out=xs[:], in_=x_rows[g * P:(g + 1) * P, :])
+        for b in range(B):
+            xs = keep.tile([P, P * L], BF16, name="x_sb%d" % b)
+            nc.sync.dma_start(out=xs[:], in_=x_rows[b])
             x_sb.append(xs)
 
-        ident = keep.tile([P, P], F32, name="ident")
+        ident = keep.tile([P, P], BF16, name="ident")
         make_identity(nc, ident[:])
-        eye = keep.tile([P, 4 * P * 4], F32, name="eye")
+        eye = keep.tile([P, 4 * NODES], F32, name="eye")
         eye_v = eye[:].rearrange("p (j q t) -> p j q t", j=4, t=4)
         nc.vector.memset(eye[:], 0.0)
-        for j in range(4):
-            nc.vector.tensor_copy(out=eye_v[:, j, :, j], in_=ident[:])
+        for t in range(4):
+            nc.vector.tensor_copy(
+                out=eye_v[:, :, 32 * t:32 * t + 32, t], in_=ident[:].rearrange("p (q j) -> p j q", j=4)
+            )
 
         al_g = keep.tile([P, 4 * NODES], BF16, name="al_g", align_bytes=64)
         al_c = keep.tile([P, NODES], U32, name="al_c", align_bytes=64)
@@ -61,98 +62,98 @@ def tile_gcn_pa_t_kernel(tc, a, x, out):
         t2_s = keep.tile([P, NODES], U8, name="t2_s", align_bytes=64)
         x_c = []
         x_s = []
-        for g in range(GROUPS):
-            xc = keep.tile([P, COLS_G], U32, name="x_c%d" % g, align_bytes=64)
-            xsc = keep.tile([P, COLS_G], U8, name="x_s%d" % g, align_bytes=64)
+        for b in range(B):
+            xc = keep.tile([P, CL], U32, name="x_c%d" % b, align_bytes=64)
+            xsc = keep.tile([P, CL], U8, name="x_s%d" % b, align_bytes=64)
             x_c.append(xc)
             x_s.append(xsc)
         weights = [(al_c, al_s), (t2_c, t2_s)]
-        busy = [0.0, 0.0]
         ctx.enter_context(tc.manual_schedule())
 
-        nc.vector.tensor_copy(
-            out=ar_g[:].rearrange("p (s q t) -> p s q t", s=4, t=4),
-            in_=a_sb[:].rearrange("p (t q s) -> p s q t", t=4, s=4),
-        )
-        a_words = a_sb[:].bitcast(F32).rearrange("q (j p u) -> q j p u", j=4, u=2)
-        al_words = al_g[:].bitcast(F32).rearrange("p (j q u) -> p j q u", j=4, u=2)
-        a_banks = []
-        for h in range(2):
-            aps = psum.tile([P, 512], F32, name="aps", tag="bank")
-            for jj in range(2):
-                for u in range(2):
-                    nc.tensor.transpose(
-                        aps[:, (2 * jj + u) * P:(2 * jj + u + 1) * P],
-                        a_words[:, 2 * h + jj, :, u],
-                        ident[:],
-                    )
-            a_banks.append(aps)
-        nc.vector.tensor_copy(
-            out=al_words[:, 0:2, :, :], in_=a_banks[0][:].rearrange("p (j u q) -> p j q u", j=2, u=2)
-        )
-        nc.scalar.copy(
-            out=al_words[:, 2:4, :, :], in_=a_banks[1][:].rearrange("p (j u q) -> p j q u", j=2, u=2)
-        )
-        nc.vector.quantize_mx(out=al_c[:].bitcast(FP8X4), scales=al_s[:], in_=al_g[:])
-        nc.vector.quantize_mx(out=ar_c[:].bitcast(FP8X4), scales=ar_s[:], in_=ar_g[:])
+        def copy_on(engine, dst, src):
+            if engine == "V":
+                nc.vector.tensor_copy(out=dst, in_=src)
+            else:
+                nc.scalar.copy(out=dst, in_=src)
 
+        x_banks = {}
         xg_of = {}
 
-        def x_bank(g, i):
-            if i == 0:
-                xg_new = xgp.tile([P, 4 * COLS_G], BF16, name="xg", align_bytes=64)
-                xg_of[g] = xg_new
-            xg_v = xg_of[g][:].rearrange("p (q l t) -> p q l t", l=L, t=4)
-            xw = x_sb[g][:].bitcast(F32).rearrange("q (p t i) -> q p t i", t=4, i=6)
-            xps = psum.tile([P, 512], F32, name="xps", tag="bank")
-            for t in range(4):
-                nc.tensor.transpose(xps[:, t * P:(t + 1) * P], xw[:, :, t, i], ident[:])
-            src = xps[:].bitcast(BF16).rearrange("p (t q e) -> p q e t", t=4, e=2)
-            nc.vector.tensor_copy(out=xg_v[:, 0:64, 2 * i:2 * i + 2, :], in_=src[:, 0:64, :, :])
-            nc.scalar.copy(out=xg_v[:, 64:128, 2 * i:2 * i + 2, :], in_=src[:, 64:128, :, :])
-            busy[0] += XHALF
-            busy[1] += XHALF
+        def x_transposes(b):
+            cols = x_sb[b][:].rearrange("r (p l) -> r l p", l=L)
+            wide = psum.tile([P, 4 * WIDE], BF16, name="xwide", tag="bank")
+            for l in range(8):
+                nc.tensor.transpose(wide[:, l * P:(l + 1) * P], cols[:, l, :], ident[:])
+            narrow = psum.tile([P, 4 * NARROW], BF16, name="xnarrow", tag="bank")
+            for l in range(8, L):
+                nc.tensor.transpose(narrow[:, (l - 8) * P:(l - 7) * P], cols[:, l, :], ident[:])
+            x_banks[b] = (wide, narrow)
 
-        def x_quant(g, half):
-            for w0, wn in (((0, 512), (512, 256)), ((768, 256), (1024, 512)))[half]:
+        def x_copies(b, engines):
+            xg = xgp.tile([P, 4 * CL], BF16, name="xg", align_bytes=64)
+            xg_of[b] = xg
+            wide, narrow = x_banks[b]
+            copy_on(engines[0], xg[:, 0:4 * WIDE], wide[:])
+            copy_on(engines[1], xg[:, 4 * WIDE:4 * CL], narrow[:])
+
+        def x_quant(b):
+            for w0, wn in ((0, WIDE), (WIDE, NARROW)):
                 nc.vector.quantize_mx(
-                    out=x_c[g][:, w0:w0 + wn].bitcast(FP8X4),
-                    scales=x_s[g][:, w0:w0 + wn],
-                    in_=xg_of[g][:, 4 * w0:4 * (w0 + wn)],
+                    out=x_c[b][:, w0:w0 + wn].bitcast(FP8X4),
+                    scales=x_s[b][:, w0:w0 + wn],
+                    in_=xg_of[b][:, 4 * w0:4 * (w0 + wn)],
                 )
-                busy[0] += 12 + 0.88 * wn
 
-        def unit(g, u):
-            term = u // B_PER_G
-            bl = u % B_PER_G
+        def unit(b, term, engines):
             wc, ws = weights[term]
-            b = g * B_PER_G + bl
             stage = stp.tile([P, 4 * CL], F32, name="stage")
             for j in range(4):
                 yps = psum.tile([P, 512], F32, name="yps", tag="bank")
-                for lo, n in ((0, 256), (256, 128)):
-                    c0 = bl * CL + lo
+                for w0, wn in ((0, WIDE), (WIDE, NARROW)):
                     nc.tensor.matmul_mx(
-                        out=yps[:, lo:lo + n],
+                        out=yps[:, w0:w0 + wn],
                         lhsT=wc[:, j * P:(j + 1) * P].bitcast(FP8X4),
                         lhsT_scale=ws[:, j * P:(j + 1) * P],
-                        rhs=x_c[g][:, c0:c0 + n].bitcast(FP8X4),
-                        rhs_scale=x_s[g][:, c0:c0 + n],
+                        rhs=x_c[b][:, w0:w0 + wn].bitcast(FP8X4),
+                        rhs_scale=x_s[b][:, w0:w0 + wn],
                         start=True,
                         stop=True,
                     )
-                if busy[0] < busy[1]:
-                    nc.vector.tensor_copy(out=stage[:, j * CL:(j + 1) * CL], in_=yps[:, 0:CL])
-                    busy[0] += YCOPY
-                else:
-                    nc.scalar.copy(out=stage[:, j * CL:(j + 1) * CL], in_=yps[:, 0:CL])
-                    busy[1] += YCOPY
+                copy_on(
+                    engines[j],
+                    stage[:, j * CL:(j + 1) * CL].rearrange("p (c l) -> p c l", l=L),
+                    yps[:, 0:CL].rearrange("p (l c) -> p c l", l=L),
+                )
             nc.sync.dma_start(
                 out=out[b, term].rearrange("(p j) c l -> p (j c l)", j=4), in_=stage[:]
             )
 
-        for i in range(6):
-            x_bank(0, i)
+        al_v = al_g[:].rearrange("p (j q t) -> p j q t", j=4, t=4)
+        a_banks = []
+        for half in range(2):
+            aps = psum.tile([P, 1024], BF16, name="aps", tag="bank")
+            for t in range(4):
+                for r in range(2):
+                    nc.tensor.transpose(
+                        aps[:, t * 256 + r * P:t * 256 + (r + 1) * P],
+                        a_sb[:, (2 * half + r) * NODES + t * P:(2 * half + r) * NODES + (t + 1) * P],
+                        ident[:],
+                    )
+            a_banks.append(aps)
+        for half in range(2):
+            copy_on(
+                "VS"[half],
+                al_v[:, :, 64 * half:64 * half + 64, :],
+                a_banks[half][:].rearrange("p (t q j) -> p j q t", t=4, j=4),
+            )
+        nc.vector.tensor_copy(
+            out=ar_g[:].rearrange("p (m t) -> p m t", t=4), in_=a_sb[:].rearrange("p (t m) -> p m t", t=4)
+        )
+        x_transposes(0)
+        nc.vector.quantize_mx(out=al_c[:].bitcast(FP8X4), scales=al_s[:], in_=al_g[:])
+        x_copies(0, "SS")
+        x_transposes(1)
+        nc.vector.quantize_mx(out=ar_c[:].bitcast(FP8X4), scales=ar_s[:], in_=ar_g[:])
 
         t2_v = t2_g[:].rearrange("p (j q t) -> p j q t", j=4, t=4)
         t_banks = []
@@ -169,7 +170,8 @@ def tile_gcn_pa_t_kernel(tc, a, x, out):
                     stop=True,
                 )
             t_banks.append(tps)
-        x_quant(0, 0)
+        x_quant(0)
+        x_copies(1, "SS")
         for j in range(4):
             nc.vector.scalar_tensor_tensor(
                 out=t2_v[:, j, :, :],
@@ -179,21 +181,20 @@ def tile_gcn_pa_t_kernel(tc, a, x, out):
                 op0=ALU.mult,
                 op1=ALU.subtract,
             )
-            busy[0] += XHALF
-        x_quant(0, 1)
+        x_quant(1)
+        unit(0, 0, "SSSS")
+        x_transposes(2)
         nc.vector.quantize_mx(out=t2_c[:].bitcast(FP8X4), scales=t2_s[:], in_=t2_g[:])
-        busy[0] += 12 + 0.88 * 512
-
-        for g in range(GROUPS):
-            more = g + 1 < GROUPS
-            for u in range(2 * B_PER_G):
-                unit(g, u)
-                pair_after = (3, 5, 6) if g == 0 else (1, 3, 5)
-                if more and u in pair_after:
-                    h = pair_after.index(u)
-                    x_bank(g + 1, 2 * h)
-                    x_bank(g + 1, 2 * h + 1)
-                    if h == 2:
-                        x_quant(g + 1, 0)
-                if more and u == pair_after[2] + 1:
-                    x_quant(g + 1, 1)
+        x_copies(2, "SV")
+        unit(1, 0, "SVSV")
+        x_quant(2)
+        unit(0, 1, "VSVS")
+        unit(1, 1, "SVSV")
+        for b in range(2, B):
+            if b + 1 < B:
+                x_transposes(b + 1)
+                x_copies(b + 1, "SV")
+            unit(b, 0, "VSVS")
+            if b + 1 < B:
+                x_quant(b + 1)
+            unit(b, 1, "SVSV")

@@ -16,8 +16,9 @@ B = 16
 C = 32
 L = 12
 CL = C * L
-WIDE = 256
-NARROW = CL - WIDE
+GROUPS = 4
+B_PER_G = 4
+COLS_G = P * L
 
 FLOPS = 2 * NODES * NODES * NODES + 2 * 2 * NODES * NODES * B * CL
 
@@ -26,7 +27,6 @@ def tile_gcn_pa_t_kernel(tc, a, x, out):
     nc = tc.nc
     with ExitStack() as ctx:
         keep = ctx.enter_context(tc.tile_pool(name="keep", bufs=1))
-        xgp = ctx.enter_context(tc.tile_pool(name="xgp", bufs=3))
         stp = ctx.enter_context(tc.tile_pool(name="stp", bufs=12))
         psum = ctx.enter_context(tc.psum_pool(name="psum", bufs=8))
 
@@ -34,21 +34,29 @@ def tile_gcn_pa_t_kernel(tc, a, x, out):
         nc.sync.dma_start(
             out=a_sb[:].rearrange("p (t m) -> p t m", t=4), in_=a.rearrange("(t p) m -> p t m", t=4)
         )
-        x_rows = x.rearrange("b c (t p) l -> b (c t) (p l)", t=4)
-        x_sb = []
-        for b in range(B):
-            xs = keep.tile([P, P * L], BF16, name="x_sb%d" % b)
-            nc.sync.dma_start(out=xs[:], in_=x_rows[b])
-            x_sb.append(xs)
+        x_by_batch = x.rearrange("b c (t p) l -> b (c t) (p l)", t=4)
+        xb_sb = []
+        for b in range(B_PER_G):
+            xs = keep.tile([P, P * L], BF16, name="xb_sb%d" % b)
+            nc.sync.dma_start(out=xs[:], in_=x_by_batch[b])
+            xb_sb.append(xs)
+        x_rows = x.rearrange("b c m l -> (b c) (m l)")
+        x_sb = {}
+        for g in range(1, GROUPS):
+            xs = keep.tile([P, NODES * L], BF16, name="x_sb%d" % g)
+            nc.sync.dma_start(out=xs[:], in_=x_rows[g * P:(g + 1) * P, :])
+            x_sb[g] = xs
 
-        ident = keep.tile([P, P], BF16, name="ident")
-        make_identity(nc, ident[:])
+        ident_bf = keep.tile([P, P], BF16, name="ident_bf")
+        make_identity(nc, ident_bf[:])
+        ident = keep.tile([P, P], F32, name="ident")
+        nc.vector.tensor_copy(out=ident[:], in_=ident_bf[:])
         eye = keep.tile([P, 4 * NODES], F32, name="eye")
         eye_v = eye[:].rearrange("p (j q t) -> p j q t", j=4, t=4)
         nc.vector.memset(eye[:], 0.0)
         for t in range(4):
             nc.vector.tensor_copy(
-                out=eye_v[:, :, 32 * t:32 * t + 32, t], in_=ident[:].rearrange("p (q j) -> p j q", j=4)
+                out=eye_v[:, :, 32 * t:32 * t + 32, t], in_=ident_bf[:].rearrange("p (q j) -> p j q", j=4)
             )
 
         al_g = keep.tile([P, 4 * NODES], BF16, name="al_g", align_bytes=64)
@@ -60,11 +68,12 @@ def tile_gcn_pa_t_kernel(tc, a, x, out):
         t2_g = keep.tile([P, 4 * NODES], BF16, name="t2_g", align_bytes=64)
         t2_c = keep.tile([P, NODES], U32, name="t2_c", align_bytes=64)
         t2_s = keep.tile([P, NODES], U8, name="t2_s", align_bytes=64)
+        xg = keep.tile([P, 4 * COLS_G], BF16, name="xg", align_bytes=64)
         x_c = []
         x_s = []
-        for b in range(B):
-            xc = keep.tile([P, CL], U32, name="x_c%d" % b, align_bytes=64)
-            xsc = keep.tile([P, CL], U8, name="x_s%d" % b, align_bytes=64)
+        for g in range(GROUPS):
+            xc = keep.tile([P, COLS_G], U32, name="x_c%d" % g, align_bytes=64)
+            xsc = keep.tile([P, COLS_G], U8, name="x_s%d" % g, align_bytes=64)
             x_c.append(xc)
             x_s.append(xsc)
         weights = [(al_c, al_s), (t2_c, t2_s)]
@@ -76,54 +85,74 @@ def tile_gcn_pa_t_kernel(tc, a, x, out):
             else:
                 nc.scalar.copy(out=dst, in_=src)
 
-        x_banks = {}
-        xg_of = {}
+        batch_banks = {}
 
-        def x_transposes(b):
-            cols = x_sb[b][:].rearrange("r (p l) -> r l p", l=L)
-            wide = psum.tile([P, 4 * WIDE], BF16, name="xwide", tag="bank")
-            for l in range(8):
-                nc.tensor.transpose(wide[:, l * P:(l + 1) * P], cols[:, l, :], ident[:])
-            narrow = psum.tile([P, 4 * NARROW], BF16, name="xnarrow", tag="bank")
-            for l in range(8, L):
-                nc.tensor.transpose(narrow[:, (l - 8) * P:(l - 7) * P], cols[:, l, :], ident[:])
-            x_banks[b] = (wide, narrow)
+        def batch_transposes(bl):
+            words = xb_sb[bl][:].bitcast(F32).rearrange("r (p i) -> r i p", i=6)
+            banks = []
+            for i0, n in ((0, 4), (4, 2)):
+                bank = psum.tile([P, n * P], F32, name="bps", tag="bank")
+                by_pair = bank[:].rearrange("p (c i t) -> p i c t", i=n, t=4)
+                for i in range(n):
+                    nc.tensor.transpose(by_pair[:, i, :, :], words[:, i0 + i, :], ident[:])
+                banks.append(bank)
+            batch_banks[bl] = banks
 
-        def x_copies(b, engines):
-            xg = xgp.tile([P, 4 * CL], BF16, name="xg", align_bytes=64)
-            xg_of[b] = xg
-            wide, narrow = x_banks[b]
-            copy_on(engines[0], xg[:, 0:4 * WIDE], wide[:])
-            copy_on(engines[1], xg[:, 4 * WIDE:4 * CL], narrow[:])
-
-        def x_quant(b):
-            for w0, wn in ((0, WIDE), (WIDE, NARROW)):
-                nc.vector.quantize_mx(
-                    out=x_c[b][:, w0:w0 + wn].bitcast(FP8X4),
-                    scales=x_s[b][:, w0:w0 + wn],
-                    in_=xg_of[b][:, 4 * w0:4 * (w0 + wn)],
+        def batch_copies(bl, engines):
+            xg_b = xg[:, bl * 4 * CL:(bl + 1) * 4 * CL].rearrange("p (c i f t) -> p c i f t", i=6, f=2, t=4)
+            for k, (i0, n) in enumerate(((0, 4), (4, 2))):
+                copy_on(
+                    engines[k],
+                    xg_b[:, :, i0:i0 + n, :, :],
+                    batch_banks[bl][k][:].bitcast(BF16).rearrange("p (c i t f) -> p c i f t", i=n, t=4, f=2),
                 )
 
-        def unit(b, term, engines):
+        def batch_quant(bl):
+            for w0, wn in ((bl * CL, 256), (bl * CL + 256, 128)):
+                nc.vector.quantize_mx(
+                    out=x_c[0][:, w0:w0 + wn].bitcast(FP8X4),
+                    scales=x_s[0][:, w0:w0 + wn],
+                    in_=xg[:, 4 * w0:4 * (w0 + wn)],
+                )
+
+        def x_bank(g, i):
+            xg_v = xg[:].rearrange("p (q l t) -> p q l t", l=L, t=4)
+            xw = x_sb[g][:].bitcast(F32).rearrange("q (t p i) -> q p t i", t=4, i=6)
+            xps = psum.tile([P, 512], F32, name="xps", tag="bank")
+            for t in range(4):
+                nc.tensor.transpose(xps[:, t * P:(t + 1) * P], xw[:, :, t, i], ident[:])
+            pairs = xps[:].bitcast(BF16).rearrange("p (t q e) -> p q e t", t=4, e=2)
+            nc.vector.tensor_copy(out=xg_v[:, 0:64, 2 * i:2 * i + 2, :], in_=pairs[:, 0:64, :, :])
+            nc.scalar.copy(out=xg_v[:, 64:128, 2 * i:2 * i + 2, :], in_=pairs[:, 64:128, :, :])
+
+        def x_quant(g, half):
+            for w0, wn in (((0, 512), (512, 256)), ((768, 256), (1024, 512)))[half]:
+                nc.vector.quantize_mx(
+                    out=x_c[g][:, w0:w0 + wn].bitcast(FP8X4),
+                    scales=x_s[g][:, w0:w0 + wn],
+                    in_=xg[:, 4 * w0:4 * (w0 + wn)],
+                )
+
+        def unit(g, u, engines):
+            term = u // B_PER_G
+            bl = u % B_PER_G
             wc, ws = weights[term]
+            b = g * B_PER_G + bl
             stage = stp.tile([P, 4 * CL], F32, name="stage")
             for j in range(4):
                 yps = psum.tile([P, 512], F32, name="yps", tag="bank")
-                for w0, wn in ((0, WIDE), (WIDE, NARROW)):
+                for lo, n in ((0, 256), (256, 128)):
+                    c0 = bl * CL + lo
                     nc.tensor.matmul_mx(
-                        out=yps[:, w0:w0 + wn],
+                        out=yps[:, lo:lo + n],
                         lhsT=wc[:, j * P:(j + 1) * P].bitcast(FP8X4),
                         lhsT_scale=ws[:, j * P:(j + 1) * P],
-                        rhs=x_c[b][:, w0:w0 + wn].bitcast(FP8X4),
-                        rhs_scale=x_s[b][:, w0:w0 + wn],
+                        rhs=x_c[g][:, c0:c0 + n].bitcast(FP8X4),
+                        rhs_scale=x_s[g][:, c0:c0 + n],
                         start=True,
                         stop=True,
                     )
-                copy_on(
-                    engines[j],
-                    stage[:, j * CL:(j + 1) * CL].rearrange("p (c l) -> p c l", l=L),
-                    yps[:, 0:CL].rearrange("p (l c) -> p c l", l=L),
-                )
+                copy_on(engines[j], stage[:, j * CL:(j + 1) * CL], yps[:, 0:CL])
             nc.sync.dma_start(
                 out=out[b, term].rearrange("(p j) c l -> p (j c l)", j=4), in_=stage[:]
             )
@@ -137,7 +166,7 @@ def tile_gcn_pa_t_kernel(tc, a, x, out):
                     nc.tensor.transpose(
                         aps[:, t * 256 + r * P:t * 256 + (r + 1) * P],
                         a_sb[:, (2 * half + r) * NODES + t * P:(2 * half + r) * NODES + (t + 1) * P],
-                        ident[:],
+                        ident_bf[:],
                     )
             a_banks.append(aps)
         for half in range(2):
@@ -149,10 +178,10 @@ def tile_gcn_pa_t_kernel(tc, a, x, out):
         nc.vector.tensor_copy(
             out=ar_g[:].rearrange("p (m t) -> p m t", t=4), in_=a_sb[:].rearrange("p (t m) -> p m t", t=4)
         )
-        x_transposes(0)
+        batch_transposes(0)
         nc.vector.quantize_mx(out=al_c[:].bitcast(FP8X4), scales=al_s[:], in_=al_g[:])
-        x_copies(0, "SS")
-        x_transposes(1)
+        batch_copies(0, "SS")
+        batch_transposes(1)
         nc.vector.quantize_mx(out=ar_c[:].bitcast(FP8X4), scales=ar_s[:], in_=ar_g[:])
 
         t2_v = t2_g[:].rearrange("p (j q t) -> p j q t", j=4, t=4)
@@ -170,8 +199,8 @@ def tile_gcn_pa_t_kernel(tc, a, x, out):
                     stop=True,
                 )
             t_banks.append(tps)
-        x_quant(0)
-        x_copies(1, "SS")
+        batch_quant(0)
+        batch_copies(1, "SS")
         for j in range(4):
             nc.vector.scalar_tensor_tensor(
                 out=t2_v[:, j, :, :],
@@ -181,20 +210,44 @@ def tile_gcn_pa_t_kernel(tc, a, x, out):
                 op0=ALU.mult,
                 op1=ALU.subtract,
             )
-        x_quant(1)
+        batch_quant(1)
         unit(0, 0, "SSSS")
-        x_transposes(2)
+        batch_transposes(2)
         nc.vector.quantize_mx(out=t2_c[:].bitcast(FP8X4), scales=t2_s[:], in_=t2_g[:])
-        x_copies(2, "SV")
-        unit(1, 0, "SVSV")
-        x_quant(2)
-        unit(0, 1, "VSVS")
-        unit(1, 1, "SVSV")
-        for b in range(2, B):
-            if b + 1 < B:
-                x_transposes(b + 1)
-                x_copies(b + 1, "SV")
-            unit(b, 0, "VSVS")
-            if b + 1 < B:
-                x_quant(b + 1)
-            unit(b, 1, "SVSV")
+        batch_copies(2, "SV")
+        unit(0, 1, "SVSV")
+        batch_quant(2)
+        unit(0, 4, "VSVS")
+        batch_transposes(3)
+        batch_copies(3, "SV")
+        unit(0, 5, "SVSV")
+        batch_quant(3)
+        unit(0, 2, "VSVS")
+        x_bank(1, 0)
+        x_bank(1, 1)
+        unit(0, 6, "VSVS")
+        x_bank(1, 2)
+        x_bank(1, 3)
+        unit(0, 3, "VSVS")
+        x_bank(1, 4)
+        x_bank(1, 5)
+        x_quant(1, 0)
+        unit(0, 7, "SSVS")
+        x_quant(1, 1)
+
+        for g in range(1, GROUPS):
+            more = g + 1 < GROUPS
+            pair_after = (1, 3, 5)
+            for u in range(2 * B_PER_G):
+                if u < 1 or (more and u == 7):
+                    unit(g, u, "SSVS")
+                else:
+                    unit(g, u, "VSVS")
+                if more and u in pair_after:
+                    h = pair_after.index(u)
+                    x_bank(g + 1, 2 * h)
+                    x_bank(g + 1, 2 * h + 1)
+                    if h == 2:
+                        x_quant(g + 1, 0)
+                if more and u == pair_after[2] + 1:
+                    x_quant(g + 1, 1)

from contextlib import ExitStack

import concourse.mybir as mybir
from concourse.masks import make_identity

F32 = mybir.dt.float32
BF16 = mybir.dt.bfloat16
U32 = mybir.dt.uint32
U8 = mybir.dt.uint8
FP8X4 = mybir.dt.float8_e4m3fn_x4
ALU = mybir.AluOpType

P = 128
NODES = 512
B = 16
C = 32
L = 12
CL = C * L
GROUPS = 4
B_PER_G = 4
COLS_G = P * L

FLOPS = 2 * NODES * NODES * NODES + 2 * 2 * NODES * NODES * B * CL


def tile_gcn_pa_t_kernel(tc, a, x, out):
    nc = tc.nc
    with ExitStack() as ctx:
        keep = ctx.enter_context(tc.tile_pool(name="keep", bufs=1))
        stp = ctx.enter_context(tc.tile_pool(name="stp", bufs=12))
        psum = ctx.enter_context(tc.psum_pool(name="psum", bufs=8))

        a_sb = keep.tile([P, 4 * NODES], BF16, name="a_sb")
        nc.sync.dma_start(
            out=a_sb[:].rearrange("p (t m) -> p t m", t=4), in_=a.rearrange("(t p) m -> p t m", t=4)
        )
        x_by_batch = x.rearrange("b c (t p) l -> b (c t) (p l)", t=4)
        xb_sb = []
        for b in range(B_PER_G):
            xs = keep.tile([P, P * L], BF16, name="xb_sb%d" % b)
            nc.sync.dma_start(out=xs[:], in_=x_by_batch[b])
            xb_sb.append(xs)
        x_rows = x.rearrange("b c m l -> (b c) (m l)")
        x_sb = {}
        for g in range(1, GROUPS):
            xs = keep.tile([P, NODES * L], BF16, name="x_sb%d" % g)
            nc.sync.dma_start(out=xs[:], in_=x_rows[g * P:(g + 1) * P, :])
            x_sb[g] = xs

        ident_bf = keep.tile([P, P], BF16, name="ident_bf")
        make_identity(nc, ident_bf[:])
        ident = keep.tile([P, P], F32, name="ident")
        nc.vector.tensor_copy(out=ident[:], in_=ident_bf[:])
        eye = keep.tile([P, 4 * NODES], F32, name="eye")
        eye_v = eye[:].rearrange("p (j q t) -> p j q t", j=4, t=4)
        nc.vector.memset(eye[:], 0.0)
        for t in range(4):
            nc.vector.tensor_copy(
                out=eye_v[:, :, 32 * t:32 * t + 32, t], in_=ident_bf[:].rearrange("p (q j) -> p j q", j=4)
            )

        al_g = keep.tile([P, 4 * NODES], BF16, name="al_g", align_bytes=64)
        al_c = keep.tile([P, NODES], U32, name="al_c", align_bytes=64)
        al_s = keep.tile([P, NODES], U8, name="al_s", align_bytes=64)
        ar_g = keep.tile([P, 4 * NODES], BF16, name="ar_g", align_bytes=64)
        ar_c = keep.tile([P, NODES], U32, name="ar_c", align_bytes=64)
        ar_s = keep.tile([P, NODES], U8, name="ar_s", align_bytes=64)
        t2_g = keep.tile([P, 4 * NODES], BF16, name="t2_g", align_bytes=64)
        t2_c = keep.tile([P, NODES], U32, name="t2_c", align_bytes=64)
        t2_s = keep.tile([P, NODES], U8, name="t2_s", align_bytes=64)
        xg = keep.tile([P, 4 * COLS_G], BF16, name="xg", align_bytes=64)
        x_c = []
        x_s = []
        for g in range(GROUPS):
            xc = keep.tile([P, COLS_G], U32, name="x_c%d" % g, align_bytes=64)
            xsc = keep.tile([P, COLS_G], U8, name="x_s%d" % g, align_bytes=64)
            x_c.append(xc)
            x_s.append(xsc)
        weights = [(al_c, al_s), (t2_c, t2_s)]
        ctx.enter_context(tc.manual_schedule())

        def copy_on(engine, dst, src):
            if engine == "V":
                nc.vector.tensor_copy(out=dst, in_=src)
            else:
                nc.scalar.copy(out=dst, in_=src)

        batch_banks = {}

        def batch_transposes(bl):
            words = xb_sb[bl][:].bitcast(F32).rearrange("r (p i) -> r i p", i=6)
            banks = []
            for i0, n in ((0, 4), (4, 2)):
                bank = psum.tile([P, n * P], F32, name="bps", tag="bank")
                by_pair = bank[:].rearrange("p (c i t) -> p i c t", i=n, t=4)
                for i in range(n):
                    nc.tensor.transpose(by_pair[:, i, :, :], words[:, i0 + i, :], ident[:])
                banks.append(bank)
            batch_banks[bl] = banks

        def batch_copies(bl, engines):
            xg_b = xg[:, bl * 4 * CL:(bl + 1) * 4 * CL].rearrange("p (c i f t) -> p c i f t", i=6, f=2, t=4)
            for k, (i0, n) in enumerate(((0, 4), (4, 2))):
                copy_on(
                    engines[k],
                    xg_b[:, :, i0:i0 + n, :, :],
                    batch_banks[bl][k][:].bitcast(BF16).rearrange("p (c i t f) -> p c i f t", i=n, t=4, f=2),
                )

        def batch_quant(bl):
            for w0, wn in ((bl * CL, 256), (bl * CL + 256, 128)):
                nc.vector.quantize_mx(
                    out=x_c[0][:, w0:w0 + wn].bitcast(FP8X4),
                    scales=x_s[0][:, w0:w0 + wn],
                    in_=xg[:, 4 * w0:4 * (w0 + wn)],
                )

        def x_bank(g, i):
            xg_v = xg[:].rearrange("p (q l t) -> p q l t", l=L, t=4)
            xw = x_sb[g][:].bitcast(F32).rearrange("q (t p i) -> q p t i", t=4, i=6)
            xps = psum.tile([P, 512], F32, name="xps", tag="bank")
            for t in range(4):
                nc.tensor.transpose(xps[:, t * P:(t + 1) * P], xw[:, :, t, i], ident[:])
            pairs = xps[:].bitcast(BF16).rearrange("p (t q e) -> p q e t", t=4, e=2)
            nc.vector.tensor_copy(out=xg_v[:, 0:64, 2 * i:2 * i + 2, :], in_=pairs[:, 0:64, :, :])
            nc.scalar.copy(out=xg_v[:, 64:128, 2 * i:2 * i + 2, :], in_=pairs[:, 64:128, :, :])

        def x_quant(g, half):
            for w0, wn in (((0, 512), (512, 256)), ((768, 256), (1024, 512)))[half]:
                nc.vector.quantize_mx(
                    out=x_c[g][:, w0:w0 + wn].bitcast(FP8X4),
                    scales=x_s[g][:, w0:w0 + wn],
                    in_=xg[:, 4 * w0:4 * (w0 + wn)],
                )

        def unit(g, u, engines):
            term = u // B_PER_G
            bl = u % B_PER_G
            wc, ws = weights[term]
            b = g * B_PER_G + bl
            stage = stp.tile([P, 4 * CL], F32, name="stage")
            for j in range(4):
                yps = psum.tile([P, 512], F32, name="yps", tag="bank")
                for lo, n in ((0, 256), (256, 128)):
                    c0 = bl * CL + lo
                    nc.tensor.matmul_mx(
                        out=yps[:, lo:lo + n],
                        lhsT=wc[:, j * P:(j + 1) * P].bitcast(FP8X4),
                        lhsT_scale=ws[:, j * P:(j + 1) * P],
                        rhs=x_c[g][:, c0:c0 + n].bitcast(FP8X4),
                        rhs_scale=x_s[g][:, c0:c0 + n],
                        start=True,
                        stop=True,
                    )
                copy_on(engines[j], stage[:, j * CL:(j + 1) * CL], yps[:, 0:CL])
            nc.sync.dma_start(
                out=out[b, term].rearrange("(p j) c l -> p (j c l)", j=4), in_=stage[:]
            )

        al_v = al_g[:].rearrange("p (j q t) -> p j q t", j=4, t=4)
        a_banks = []
        for half in range(2):
            aps = psum.tile([P, 1024], BF16, name="aps", tag="bank")
            for t in range(4):
                for r in range(2):
                    nc.tensor.transpose(
                        aps[:, t * 256 + r * P:t * 256 + (r + 1) * P],
                        a_sb[:, (2 * half + r) * NODES + t * P:(2 * half + r) * NODES + (t + 1) * P],
                        ident_bf[:],
                    )
            a_banks.append(aps)
        for half in range(2):
            copy_on(
                "VS"[half],
                al_v[:, :, 64 * half:64 * half + 64, :],
                a_banks[half][:].rearrange("p (t q j) -> p j q t", t=4, j=4),
            )
        nc.vector.tensor_copy(
            out=ar_g[:].rearrange("p (m t) -> p m t", t=4), in_=a_sb[:].rearrange("p (t m) -> p m t", t=4)
        )
        batch_transposes(0)
        nc.vector.quantize_mx(out=al_c[:].bitcast(FP8X4), scales=al_s[:], in_=al_g[:])
        batch_copies(0, "SS")
        batch_transposes(1)
        nc.vector.quantize_mx(out=ar_c[:].bitcast(FP8X4), scales=ar_s[:], in_=ar_g[:])

        t2_v = t2_g[:].rearrange("p (j q t) -> p j q t", j=4, t=4)
        t_banks = []
        for j in range(4):
            tps = psum.tile([P, 512], F32, name="tps", tag="bank")
            for s in range(4):
                nc.tensor.matmul_mx(
                    out=tps[:, s * P:(s + 1) * P],
                    lhsT=ar_c[:, s * P:(s + 1) * P].bitcast(FP8X4),
                    lhsT_scale=ar_s[:, s * P:(s + 1) * P],
                    rhs=al_c[:, j * P:(j + 1) * P].bitcast(FP8X4),
                    rhs_scale=al_s[:, j * P:(j + 1) * P],
                    start=True,
                    stop=True,
                )
            t_banks.append(tps)
        batch_quant(0)
        batch_copies(1, "SS")
        for j in range(4):
            nc.vector.scalar_tensor_tensor(
                out=t2_v[:, j, :, :],
                in0=t_banks[j][:].rearrange("p (t q) -> p q t", t=4),
                scalar=2.0,
                in1=eye_v[:, j, :, :],
                op0=ALU.mult,
                op1=ALU.subtract,
            )
        batch_quant(1)
        unit(0, 0, "SSSS")
        batch_transposes(2)
        nc.vector.quantize_mx(out=t2_c[:].bitcast(FP8X4), scales=t2_s[:], in_=t2_g[:])
        batch_copies(2, "SV")
        unit(0, 1, "SVSV")
        batch_quant(2)
        unit(0, 4, "VSVS")
        batch_transposes(3)
        batch_copies(3, "SV")
        unit(0, 5, "SVSV")
        batch_quant(3)
        unit(0, 2, "VSVS")
        x_bank(1, 0)
        x_bank(1, 1)
        unit(0, 6, "VSVS")
        x_bank(1, 2)
        x_bank(1, 3)
        unit(0, 3, "VSVS")
        x_bank(1, 4)
        x_bank(1, 5)
        x_quant(1, 0)
        unit(0, 7, "SSVS")
        x_quant(1, 1)

        for g in range(1, GROUPS):
            more = g + 1 < GROUPS
            pair_after = (1, 3, 5)
            for u in range(2 * B_PER_G):
                if u < 1 or (more and u == 7):
                    unit(g, u, "SSVS")
                else:
                    unit(g, u, "VSVS")
                if more and u in pair_after:
                    h = pair_after.index(u)
                    x_bank(g + 1, 2 * h)
                    x_bank(g + 1, 2 * h + 1)
                    if h == 2:
                        x_quant(g + 1, 0)
                if more and u == pair_after[2] + 1:
                    x_quant(g + 1, 1)
